import numpy as np
import ml_dtypes


def mxq(x, axis, fmt="e4m3"):
    dtype, down = {"e4m3": (ml_dtypes.float8_e4m3fn, 7), "e5m2": (ml_dtypes.float8_e5m2, 14)}[fmt]
    v = np.moveaxis(np.asarray(x, np.float32).astype(ml_dtypes.bfloat16).astype(np.float64), axis, -1)
    blocks = v.reshape(v.shape[:-1] + (-1, 32))
    amax = np.abs(blocks).max(-1, keepdims=True)
    byte = np.maximum(np.where(amax > 0, np.frexp(amax)[1] - 1 + 127, 0) - down, 1)
    scale = np.exp2(byte - 127.0)
    codes = (blocks / scale).astype(np.float32).astype(dtype).astype(np.float64)
    return np.moveaxis((codes * scale).reshape(v.shape), -1, axis)


WIDE = False


def mx_kscale(k):
    if not WIDE:
        return np.ones(k)
    levels = np.array([10, -10, 5, -5, 0])
    a = np.random.permutation(np.resize(levels, k // 512 * 4)).reshape(k // 512, 4)
    idx = np.arange(k)
    return np.exp2(a[idx // 512, idx % 128 // 32])


BF16 = ml_dtypes.bfloat16


def bf(x):
    return np.asarray(x, np.float32).astype(BF16)


def f64(x):
    return np.asarray(x).astype(np.float64)


E2M1 = np.array([0.0, 0.5, 1.0, 1.5, 2.0, 3.0, 4.0, 6.0, -0.0, -0.5, -1.0, -1.5, -2.0, -3.0, -4.0, -6.0])


def pack_weight(w, fmt):
    k, n = w.shape
    w = f64(bf(w)).reshape(k // 32, 32, n)
    amax = np.abs(w).max(1)
    if fmt == "e4m3":
        byte = np.frexp(amax)[1] - 1 + 127 - 7
    else:
        mant, ex = np.frexp(amax / 6.0)
        byte = np.where(mant > 0.5, ex, ex - 1) + 127
    byte = np.clip(np.where(amax > 0, byte, 1), 1, 254)
    scaled = (w * np.exp2(127.0 - byte)[:, None, :]).reshape(k, n).astype(np.float32)
    by_word = np.ascontiguousarray(scaled.reshape(k // 512, 128, 4, n).transpose(0, 1, 3, 2))
    if fmt == "e4m3":
        words = by_word.astype(ml_dtypes.float8_e4m3fn).view(np.uint8)
    else:
        c = by_word.astype(ml_dtypes.float4_e2m1fn).view(np.uint8) & 0xF
        words = c[..., 0::2] | (c[..., 1::2] << 4)
    return np.ascontiguousarray(words), np.ascontiguousarray(byte.astype(np.uint8).reshape(k // 512, 16, n))


def unpack_weight(words, scales, fmt):
    g, p, n, _ = words.shape
    if fmt == "e4m3":
        vals = np.ascontiguousarray(words).view(ml_dtypes.float8_e4m3fn).astype(np.float64)
    else:
        nib = np.empty((g, p, n, 4), np.uint8)
        nib[..., 0::2] = words & 0xF
        nib[..., 1::2] = words >> 4
        vals = E2M1[nib]
    vals = vals * np.repeat(np.exp2(scales.astype(np.float64) - 127.0), 8, axis=1)[..., None]
    return vals.transpose(0, 1, 3, 2).reshape(g * 512, n)


B, I, N, L = 128, 2048, 1536, 2
SIGSIZE = sum(2 ** k for k in range(1, L + 1))
SAVED = N * (1 + SIGSIZE)


def sigjoin(prev_sigs, disp, time_lapse, level):
    n = prev_sigs.shape[0]
    v = np.concatenate([disp, np.full_like(disp, 1.0) * time_lapse], axis=1)
    seg = [v]
    for k in range(2, level + 1):
        seg.append((seg[-1][:, :, None] * v[:, None, :]).reshape(n, -1) / k)
    S, off = [], 0
    for k in range(1, level + 1):
        sz = 2 ** k
        S.append(prev_sigs[:, off:off + sz])
        off += sz
    out = []
    for k in range(1, level + 1):
        r = S[k - 1] + seg[k - 1]
        for i in range(1, k):
            r = r + (S[i - 1][:, :, None] * seg[k - i - 1][:, None, :]).reshape(n, 2 ** k)
        out.append(r)
    return np.concatenate(out, axis=1)


def setup_inputs():
    s = mx_kscale(I)
    u = mx_kscale(SAVED)
    d = np.minimum(u, 1.0 / u) ** 2
    x = bf(np.random.standard_normal((B, I)) * s)
    prev_sigs = bf(np.random.standard_normal((B, N * SIGSIZE)) * 0.5 * d[:N * SIGSIZE])
    prev_states = bf(np.random.standard_normal((B, N)) * d[N * SIGSIZE:])
    W_w_words, W_w_scales = pack_weight(np.ascontiguousarray((np.random.standard_normal((N, I)) / np.sqrt(I) / s).T), "e4m3")
    W_b = bf(np.random.standard_normal(N) * 0.1)
    U_w_words, U_w_scales = pack_weight(np.ascontiguousarray((np.random.standard_normal((N, SAVED)) / np.sqrt(SAVED) / d).T), "e4m3")
    U_b = bf(np.random.standard_normal(N) * 0.1)
    log_timelapse = bf(np.log(0.1) + 0.2 * np.random.standard_normal(1))
    return {"x": x,
            "prev_sigs": prev_sigs,
            "prev_states": prev_states,
            "W_w_words": W_w_words,
            "W_w_scales": W_w_scales,
            "W_b": W_b,
            "U_w_words": U_w_words,
            "U_w_scales": U_w_scales,
            "U_b": U_b,
            "log_timelapse": log_timelapse}


def reference(x, prev_sigs, prev_states, W_w_words, W_w_scales, W_b, U_w_words, U_w_scales, U_b, log_timelapse):
    h = (mxq(f64(x), 1, "e4m3") @ unpack_weight(W_w_words, W_w_scales, "e4m3")) + f64(W_b)
    mem = np.concatenate([f64(prev_sigs), f64(prev_states)], 1)
    raw = h + (mxq(mem, 1, "e4m3") @ unpack_weight(U_w_words, U_w_scales, "e4m3")) + f64(U_b)
    disp = (raw - f64(prev_states)).reshape(-1, 1)
    tl = np.exp(f64(log_timelapse))[0]
    sigs = sigjoin(f64(prev_sigs).reshape(-1, SIGSIZE), disp, tl, L)
    sigs = sigs.reshape(-1, N * SIGSIZE)
    return np.concatenate([sigs, raw], axis=1)

@@ -1,0 +1,199 @@
+from contextlib import ExitStack
+
+import concourse.mybir as mybir
+from concourse.masks import make_identity
+
+F32 = mybir.dt.float32
+BF16 = mybir.dt.bfloat16
+I32 = mybir.dt.int32
+U32 = mybir.dt.uint32
+U8 = mybir.dt.uint8
+FP8X4 = mybir.dt.float8_e4m3fn_x4
+ALU = mybir.AluOpType
+ACT = mybir.ActivationFunctionType
+
+P = 128
+IN = 2048
+UNITS = 1536
+SIG = 6
+KTOT = IN + UNITS * (SIG + 1)
+GROUPS = KTOT // 512
+WG = IN // 512
+CH = 512
+NCH = UNITS // CH
+TAILG = 12
+PERT = 3
+FULLG = GROUPS - TAILG
+LOOK = 8
+FLOPS = 2 * P * KTOT * UNITS
+
+
+def tile_recurrentsig_w_kernel(
+    tc, x, prev_sigs, prev_states, W_w_words, W_w_scales, W_b, U_w_words, U_w_scales, U_b, log_timelapse, out
+):
+    nc = tc.nc
+    with ExitStack() as ctx:
+        keep = ctx.enter_context(tc.tile_pool(name="keep", bufs=1))
+        stage = ctx.enter_context(tc.tile_pool(name="stage", bufs=4))
+        wpool = ctx.enter_context(tc.tile_pool(name="wpool", bufs=10))
+        tpool = ctx.enter_context(tc.psum_pool(name="tpool", bufs=5))
+        zpool = ctx.enter_context(tc.psum_pool(name="zpool", bufs=1))
+
+        planes = keep.tile([P, 7, UNITS], U8, align_bytes=64)
+        nc.vector.memset(planes[:].rearrange("p t n -> p (t n)").bitcast(I32), 0)
+        ident = keep.tile([P, P], F32)
+        make_identity(nc, ident[:])
+        ones = keep.tile([P, P], BF16)
+        nc.gpsimd.memset(ones[:], 1.0)
+        bias_rows = keep.tile([P, UNITS], BF16)
+        nc.gpsimd.memset(bias_rows[:], 0.0)
+        ltl = keep.tile([P, 1], BF16)
+        nc.scalar.dma_start(out=ltl[:], in_=log_timelapse.partition_broadcast(P))
+        nc.scalar.dma_start(out=bias_rows[0:1, :], in_=W_b.rearrange("(o n) -> o n", o=1))
+        nc.scalar.dma_start(out=bias_rows[1:2, :], in_=U_b.rearrange("(o n) -> o n", o=1))
+
+        acts = keep.tile([P, KTOT], BF16, align_bytes=64)
+        nc.sync.dma_start(out=acts[:, 0:IN], in_=x)
+        for s in range(3):
+            nc.sync.dma_start(
+                out=acts[:, IN + 3072 * s : IN + 3072 * (s + 1)], in_=prev_sigs[:, 3072 * s : 3072 * (s + 1)]
+            )
+        nc.sync.dma_start(out=acts[:, IN + UNITS * SIG : KTOT], in_=prev_states)
+        sigs = acts[:, IN : IN + UNITS * SIG].rearrange("p (n j) -> p n j", j=SIG)
+        states = acts[:, IN + UNITS * SIG : KTOT]
+
+        for t in range(7):
+            for q in range(4):
+                if t == 0:
+                    src = W_w_scales[0:4, 4 * q : 4 * q + 4, :]
+                    rows = 16
+                elif t < 6:
+                    src = U_w_scales[4 * (t - 1) : 4 * t, 4 * q : 4 * q + 4, :]
+                    rows = 16
+                else:
+                    src = U_w_scales[20, 4 * q : 4 * q + 4, :]
+                    rows = 4
+                nc.sync.dma_start(out=planes[32 * q : 32 * q + rows, t, :].bitcast(I32), in_=src.bitcast(I32))
+
+        a_codes = keep.tile([P, GROUPS * P], U32, align_bytes=64)
+        a_scales = keep.tile([P, GROUPS * P], U8, align_bytes=64)
+        acts_w = acts[:].bitcast(F32)
+        regrouped = []
+
+        def quantise(i):
+            ng, grouped = regrouped[i]
+            nc.vector.quantize_mx(
+                out=a_codes[:, 256 * i : 256 * i + P * ng].bitcast(FP8X4),
+                scales=a_scales[:, 256 * i : 256 * i + P * ng],
+                in_=grouped[:, 0:ng].rearrange("p g b t -> p (g b t)"),
+            )
+
+        for i in range((GROUPS + 1) // 2):
+            ng = min(2, GROUPS - 2 * i)
+            tp = tpool.tile([P, 2, 2, P], F32, tag="tp")
+            for gi in range(ng):
+                g = 2 * i + gi
+                for u in range(2):
+                    nc.tensor.transpose(tp[:, gi, u, :], acts_w[:, 256 * g + u : 256 * (g + 1) : 2], ident[:])
+            grouped = stage.tile([P, 2, P, 4], BF16, align_bytes=64, tag="grouped")
+            dst = grouped[:, 0:ng].bitcast(F32)
+            src = tp[:, 0:ng].rearrange("p g u b -> p g b u")
+            if i % 2 == 0:
+                nc.vector.tensor_copy(out=dst, in_=src)
+            else:
+                nc.scalar.copy(out=dst, in_=src)
+            regrouped.append((ng, grouped))
+            if i > 0:
+                quantise(i - 1)
+        quantise((GROUPS + 1) // 2 - 1)
+
+        tl = keep.tile([P, 1], F32)
+        nc.scalar.activation(out=tl[:], in_=ltl[:], func=ACT.Exp)
+        tlh = keep.tile([P, 1], F32)
+        nc.scalar.mul(out=tlh[:], in_=tl[:], mul=0.5)
+        bias_b = keep.tile([P, UNITS], F32)
+        for c in range(NCH):
+            bp = tpool.tile([P, CH], F32, tag="tp")
+            nc.tensor.matmul(out=bp[:], lhsT=ones[:], rhs=bias_rows[:, CH * c : CH * (c + 1)], start=True, stop=True)
+            nc.scalar.copy(out=bias_b[:, CH * c : CH * (c + 1)], in_=bp[:])
+        c4 = keep.tile([P, UNITS], F32)
+        nc.scalar.activation(out=c4[:], in_=sigs[:, :, 1], func=ACT.Identity, bias=tlh[:, 0:1], scale=1.0)
+        incs = []
+        for c in range(NCH):
+            inc = keep.tile([P, SIG, CH], F32, name="inc%d" % c)
+            cols = slice(CH * c, CH * (c + 1))
+            nc.scalar.activation(out=inc[:, 1, :], in_=sigs[:, cols, 1], func=ACT.Identity, bias=tl[:, 0:1], scale=0.0)
+            nc.scalar.activation(out=inc[:, 5, :], in_=c4[:, cols], func=ACT.Copy, scale=tl[:, 0:1])
+            incs.append(inc)
+
+        z = [zpool.tile([P, CH], F32, name="z%d" % c) for c in range(NCH)]
+        rout = keep.tile([P, UNITS], F32)
+
+        def mx_pass(g, c, rhs):
+            k = 4 * (g % 4)
+            nc.tensor.matmul_mx(
+                out=z[c][:],
+                lhsT=a_codes[:, P * g : P * (g + 1)].bitcast(FP8X4),
+                lhsT_scale=a_scales[:, P * g : P * (g + 1)],
+                rhs=rhs.bitcast(FP8X4),
+                rhs_scale=planes[k:P, g // 4, CH * c : CH * (c + 1)],
+                start=(g == 0),
+                stop=(g == GROUPS - 1),
+            )
+
+        def epilogue(c):
+            cols = slice(CH * c, CH * (c + 1))
+            inc = incs[c]
+            d = inc[:, 0, :]
+            nc.vector.tensor_tensor(out=rout[:, cols], in0=z[c][:], in1=bias_b[:, cols], op=ALU.add)
+            nc.vector.tensor_tensor(out=d, in0=rout[:, cols], in1=states[:, cols], op=ALU.subtract)
+            half = stage.tile([P, CH], F32, tag="half", bufs=2)
+            nc.vector.scalar_tensor_tensor(
+                out=half[:], in0=d, scalar=0.5, in1=sigs[:, cols, 0], op0=ALU.mult, op1=ALU.add
+            )
+            nc.scalar.activation(out=inc[:, 3, :], in_=half[:], func=ACT.Copy, scale=tl[:, 0:1])
+            nc.vector.tensor_tensor(out=inc[:, 2, :], in0=d, in1=half[:], op=ALU.mult)
+            nc.vector.tensor_tensor(out=inc[:, 4, :], in0=d, in1=c4[:, cols], op=ALU.mult)
+            osig = keep.tile([P, CH, SIG], F32, name="osig%d" % c)
+            nc.vector.tensor_tensor(
+                out=osig[:], in0=inc[:].rearrange("p j n -> p n j"), in1=sigs[:, cols, :], op=ALU.add
+            )
+            nc.sync.dma_start(out=out[:, UNITS * SIG + CH * c : UNITS * SIG + CH * (c + 1)], in_=rout[:, cols])
+            nc.sync.dma_start(
+                out=out[:, CH * SIG * c : CH * SIG * (c + 1)], in_=osig[:].rearrange("p n j -> p (n j)")
+            )
+
+        plan = [("full", g, 0) for g in range(FULLG)]
+        plan += [("tail", FULLG + PERT * j, c) for c in range(NCH) for j in range(TAILG // PERT)]
+        tiles = []
+
+        def load(i):
+            kind, g, c = plan[i]
+            if kind == "full":
+                wt = wpool.tile([P, UNITS], U32, align_bytes=64, tag="wt")
+                words = W_w_words[g] if g < WG else U_w_words[g - WG]
+                nc.sync.dma_start(out=wt[:].bitcast(I32), in_=words.rearrange("p n t -> p (n t)").bitcast(I32))
+            else:
+                wt = wpool.tile([P, PERT, CH], U32, align_bytes=64, tag="wt")
+                nc.sync.dma_start(
+                    out=wt[:].bitcast(I32),
+                    in_=U_w_words[g - WG : g - WG + PERT, :, CH * c : CH * (c + 1), :]
+                    .rearrange("g p n t -> p g (n t)")
+                    .bitcast(I32),
+                )
+            tiles.append(wt)
+
+        for i in range(LOOK):
+            load(i)
+        for i in range(len(plan)):
+            if i + LOOK < len(plan):
+                load(i + LOOK)
+            kind, g, c = plan[i]
+            if kind == "full":
+                for cc in range(NCH):
+                    mx_pass(g, cc, tiles[i][:, CH * cc : CH * (cc + 1)])
+            else:
+                for gi in range(PERT):
+                    mx_pass(g + gi, c, tiles[i][:, gi, :])
+                if g + PERT == GROUPS:
+                    epilogue(c)

@@ -35,7 +35,7 @@ def tile_recurrentsig_w_kernel(
     with ExitStack() as ctx:
         keep = ctx.enter_context(tc.tile_pool(name="keep", bufs=1))
         stage = ctx.enter_context(tc.tile_pool(name="stage", bufs=4))
-        wpool = ctx.enter_context(tc.tile_pool(name="wpool", bufs=10))
+        wpool = ctx.enter_context(tc.tile_pool(name="wpool", bufs=9))
         tpool = ctx.enter_context(tc.psum_pool(name="tpool", bufs=5))
         zpool = ctx.enter_context(tc.psum_pool(name="zpool", bufs=1))
 
@@ -116,15 +116,21 @@ def tile_recurrentsig_w_kernel(
             bp = tpool.tile([P, CH], F32, tag="tp")
             nc.tensor.matmul(out=bp[:], lhsT=ones[:], rhs=bias_rows[:, CH * c : CH * (c + 1)], start=True, stop=True)
             nc.scalar.copy(out=bias_b[:, CH * c : CH * (c + 1)], in_=bp[:])
-        c4 = keep.tile([P, UNITS], F32)
-        nc.scalar.activation(out=c4[:], in_=sigs[:, :, 1], func=ACT.Identity, bias=tlh[:, 0:1], scale=1.0)
-        incs = []
+        vps, wps, pps = [], [], []
         for c in range(NCH):
-            inc = keep.tile([P, SIG, CH], F32, name="inc%d" % c)
             cols = slice(CH * c, CH * (c + 1))
-            nc.scalar.activation(out=inc[:, 1, :], in_=sigs[:, cols, 1], func=ACT.Identity, bias=tl[:, 0:1], scale=0.0)
-            nc.scalar.activation(out=inc[:, 5, :], in_=c4[:, cols], func=ACT.Copy, scale=tl[:, 0:1])
-            incs.append(inc)
+            vp = keep.tile([P, 2, CH], F32, name="vp%d" % c)
+            wp = keep.tile([P, 2, CH], F32, name="wp%d" % c)
+            pp = keep.tile([P, 3, CH, 2], F32, name="pp%d" % c)
+            nc.scalar.activation(out=wp[:, 1, :], in_=sigs[:, cols, 1], func=ACT.Identity, bias=tlh[:, 0:1], scale=1.0)
+            nc.scalar.activation(out=vp[:, 1, :], in_=sigs[:, cols, 1], func=ACT.Identity, bias=tl[:, 0:1], scale=0.0)
+            nc.scalar.activation(
+                out=pp[:, 0, :, 1], in_=sigs[:, cols, 1], func=ACT.Identity, bias=tl[:, 0:1], scale=0.0
+            )
+            vps.append(vp)
+            wps.append(wp)
+            pps.append(pp)
+        sig4 = acts[:, IN : IN + UNITS * SIG].rearrange("p (n k e) -> p n k e", k=3, e=2)
 
         z = [zpool.tile([P, CH], F32, name="z%d" % c) for c in range(NCH)]
         rout = keep.tile([P, UNITS], F32)
@@ -141,27 +147,38 @@ def tile_recurrentsig_w_kernel(
                 stop=(g == GROUPS - 1),
             )
 
-        def epilogue(c):
-            cols = slice(CH * c, CH * (c + 1))
-            inc = incs[c]
-            d = inc[:, 0, :]
-            nc.vector.tensor_tensor(out=rout[:, cols], in0=z[c][:], in1=bias_b[:, cols], op=ALU.add)
-            nc.vector.tensor_tensor(out=d, in0=rout[:, cols], in1=states[:, cols], op=ALU.subtract)
-            half = stage.tile([P, CH], F32, tag="half", bufs=2)
-            nc.vector.scalar_tensor_tensor(
-                out=half[:], in0=d, scalar=0.5, in1=sigs[:, cols, 0], op0=ALU.mult, op1=ALU.add
-            )
-            nc.scalar.activation(out=inc[:, 3, :], in_=half[:], func=ACT.Copy, scale=tl[:, 0:1])
-            nc.vector.tensor_tensor(out=inc[:, 2, :], in0=d, in1=half[:], op=ALU.mult)
-            nc.vector.tensor_tensor(out=inc[:, 4, :], in0=d, in1=c4[:, cols], op=ALU.mult)
-            osig = keep.tile([P, CH, SIG], F32, name="osig%d" % c)
-            nc.vector.tensor_tensor(
-                out=osig[:], in0=inc[:].rearrange("p j n -> p n j"), in1=sigs[:, cols, :], op=ALU.add
-            )
-            nc.sync.dma_start(out=out[:, UNITS * SIG + CH * c : UNITS * SIG + CH * (c + 1)], in_=rout[:, cols])
-            nc.sync.dma_start(
-                out=out[:, CH * SIG * c : CH * SIG * (c + 1)], in_=osig[:].rearrange("p n j -> p (n j)")
-            )
+        def epilogue(c, parts):
+            vp, wp, pp = vps[c], wps[c], pps[c]
+            osig = keep.tile([P, CH, 3, 2], F32, name="osig%d" % c)
+            w = CH // parts
+            whole = slice(CH * c, CH * (c + 1))
+            nc.vector.tensor_tensor(out=rout[:, whole], in0=z[c][:], in1=bias_b[:, whole], op=ALU.add)
+            nc.sync.dma_start(out=out[:, UNITS * SIG + CH * c : UNITS * SIG + CH * (c + 1)], in_=rout[:, whole])
+            for h in range(parts):
+                loc = slice(w * h, w * (h + 1))
+                cols = slice(CH * c + w * h, CH * c + w * (h + 1))
+                d = vp[:, 0, loc]
+                nc.vector.tensor_tensor(out=d, in0=rout[:, cols], in1=states[:, cols], op=ALU.subtract)
+                nc.scalar.copy(out=pp[:, 0, loc, 0], in_=d)
+                nc.vector.scalar_tensor_tensor(
+                    out=wp[:, 0, loc], in0=d, scalar=0.5, in1=sigs[:, cols, 0], op0=ALU.mult, op1=ALU.add
+                )
+                nc.vector.tensor_tensor(
+                    out=pp[:, 1:3, loc, :],
+                    in0=wp[:, :, loc].unsqueeze(3).to_broadcast([P, 2, w, 2]),
+                    in1=vp[:, :, loc].rearrange("p j n -> p n j").unsqueeze(1).to_broadcast([P, 2, w, 2]),
+                    op=ALU.mult,
+                )
+                nc.vector.tensor_tensor(
+                    out=osig[:, loc, :, :],
+                    in0=pp[:, :, loc, :].rearrange("p k n e -> p n k e"),
+                    in1=sig4[:, cols, :, :],
+                    op=ALU.add,
+                )
+                nc.sync.dma_start(
+                    out=out[:, SIG * (CH * c + w * h) : SIG * (CH * c + w * (h + 1))],
+                    in_=osig[:, loc, :, :].rearrange("p n k e -> p (n k e)"),
+                )
 
         plan = [("full", g, 0) for g in range(FULLG)]
         plan += [("tail", FULLG + PERT * j, c) for c in range(NCH) for j in range(TAILG // PERT)]
@@ -196,4 +213,4 @@ def tile_recurrentsig_w_kernel(
                 for gi in range(PERT):
                     mx_pass(g + gi, c, tiles[i][:, gi, :])
                 if g + PERT == GROUPS:
-                    epilogue(c)
+                    epilogue(c, 2 if c == NCH - 1 else 1)

@@ -39,14 +39,14 @@ def tile_recurrentsig_w_kernel(
         tpool = ctx.enter_context(tc.psum_pool(name="tpool", bufs=5))
         zpool = ctx.enter_context(tc.psum_pool(name="zpool", bufs=1))
 
+        bias_rows = keep.tile([P, UNITS], BF16)
+        nc.vector.memset(bias_rows[:], 0.0)
         planes = keep.tile([P, 7, UNITS], U8, align_bytes=64)
         nc.vector.memset(planes[:].rearrange("p t n -> p (t n)").bitcast(I32), 0)
+        ones = keep.tile([P, P], BF16)
+        nc.vector.memset(ones[:], 1.0)
         ident = keep.tile([P, P], F32)
         make_identity(nc, ident[:])
-        ones = keep.tile([P, P], BF16)
-        nc.gpsimd.memset(ones[:], 1.0)
-        bias_rows = keep.tile([P, UNITS], BF16)
-        nc.gpsimd.memset(bias_rows[:], 0.0)
         ltl = keep.tile([P, 1], BF16)
         nc.scalar.dma_start(out=ltl[:], in_=log_timelapse.partition_broadcast(P))
         nc.scalar.dma_start(out=bias_rows[0:1, :], in_=W_b.rearrange("(o n) -> o n", o=1))
@@ -62,18 +62,20 @@ def tile_recurrentsig_w_kernel(
         sigs = acts[:, IN : IN + UNITS * SIG].rearrange("p (n j) -> p n j", j=SIG)
         states = acts[:, IN + UNITS * SIG : KTOT]
 
-        for t in range(7):
-            for q in range(4):
-                if t == 0:
-                    src = W_w_scales[0:4, 4 * q : 4 * q + 4, :]
-                    rows = 16
-                elif t < 6:
-                    src = U_w_scales[4 * (t - 1) : 4 * t, 4 * q : 4 * q + 4, :]
-                    rows = 16
-                else:
-                    src = U_w_scales[20, 4 * q : 4 * q + 4, :]
-                    rows = 4
-                nc.sync.dma_start(out=planes[32 * q : 32 * q + rows, t, :].bitcast(I32), in_=src.bitcast(I32))
+        for q in range(4):
+            nc.sync.dma_start(
+                out=planes[32 * q : 32 * q + 16, 0, :].bitcast(I32), in_=W_w_scales[0:4, 4 * q : 4 * q + 4, :].bitcast(I32)
+            )
+        for q in range(4):
+            nc.sync.dma_start(
+                out=planes[32 * q : 32 * q + 4, 6, :].bitcast(I32), in_=U_w_scales[20, 4 * q : 4 * q + 4, :].bitcast(I32)
+            )
+        by_row = U_w_scales[0:20].rearrange("(t k) q n -> q k t n", k=4)
+        for q in range(4):
+            for r in range(4):
+                nc.gpsimd.dma_start(
+                    out=planes[32 * q + r : 32 * q + 16 : 4, 1:6, :].bitcast(F32), in_=by_row[4 * q + r].bitcast(F32)
+                )
 
         a_codes = keep.tile([P, GROUPS * P], U32, align_bytes=64)
         a_scales = keep.tile([P, GROUPS * P], U8, align_bytes=64)

@@ -24,6 +24,7 @@ NCH = UNITS // CH
 TAILG = 12
 PERT = 3
 FULLG = GROUPS - TAILG
+HWT = 3
 LOOK = 8
 FLOPS = 2 * P * KTOT * UNITS
 
@@ -62,20 +63,23 @@ def tile_recurrentsig_w_kernel(
         sigs = acts[:, IN : IN + UNITS * SIG].rearrange("p (n j) -> p n j", j=SIG)
         states = acts[:, IN + UNITS * SIG : KTOT]
 
-        for q in range(4):
-            nc.sync.dma_start(
-                out=planes[32 * q : 32 * q + 16, 0, :].bitcast(I32), in_=W_w_scales[0:4, 4 * q : 4 * q + 4, :].bitcast(I32)
-            )
-        for q in range(4):
-            nc.sync.dma_start(
-                out=planes[32 * q : 32 * q + 4, 6, :].bitcast(I32), in_=U_w_scales[20, 4 * q : 4 * q + 4, :].bitcast(I32)
-            )
-        by_row = U_w_scales[0:20].rearrange("(t k) q n -> q k t n", k=4)
+        for t in range(HWT):
+            for q in range(4):
+                if t == 0:
+                    src = W_w_scales[0:4, 4 * q : 4 * q + 4, :]
+                else:
+                    src = U_w_scales[4 * (t - 1) : 4 * t, 4 * q : 4 * q + 4, :]
+                nc.sync.dma_start(out=planes[32 * q : 32 * q + 16, t, :].bitcast(I32), in_=src.bitcast(I32))
+        by_row = U_w_scales[4 * (HWT - 1) : 20].rearrange("(t k) q n -> q k t n", k=4)
         for q in range(4):
             for r in range(4):
                 nc.gpsimd.dma_start(
-                    out=planes[32 * q + r : 32 * q + 16 : 4, 1:6, :].bitcast(F32), in_=by_row[4 * q + r].bitcast(F32)
+                    out=planes[32 * q + r : 32 * q + 16 : 4, HWT:6, :].bitcast(F32), in_=by_row[4 * q + r].bitcast(F32)
                 )
+        for q in range(4):
+            nc.gpsimd.dma_start(
+                out=planes[32 * q : 32 * q + 4, 6, :].bitcast(F32), in_=U_w_scales[20, 4 * q : 4 * q + 4, :].bitcast(F32)
+            )
 
         a_codes = keep.tile([P, GROUPS * P], U32, align_bytes=64)
         a_scales = keep.tile([P, GROUPS * P], U8, align_bytes=64)

@@ -42,8 +42,10 @@ def tile_recurrentsig_w_kernel(
 
         bias_rows = keep.tile([P, UNITS], BF16)
         nc.vector.memset(bias_rows[:], 0.0)
-        planes = keep.tile([P, 7, UNITS], U8, align_bytes=64)
+        planes = keep.tile([P, HWT, UNITS], U8, align_bytes=64)
         nc.vector.memset(planes[:].rearrange("p t n -> p (t n)").bitcast(I32), 0)
+        late = keep.tile([P, 7 - HWT, UNITS], U8, align_bytes=64)
+        nc.vector.memset(late[:].rearrange("p t n -> p (t n)").bitcast(I32), 0)
         ones = keep.tile([P, P], BF16)
         nc.vector.memset(ones[:], 1.0)
         ident = keep.tile([P, P], F32)
@@ -74,11 +76,11 @@ def tile_recurrentsig_w_kernel(
         for q in range(4):
             for r in range(4):
                 nc.gpsimd.dma_start(
-                    out=planes[32 * q + r : 32 * q + 16 : 4, HWT:6, :].bitcast(F32), in_=by_row[4 * q + r].bitcast(F32)
+                    out=late[32 * q + r : 32 * q + 16 : 4, 0 : 6 - HWT, :].bitcast(F32), in_=by_row[4 * q + r].bitcast(F32)
                 )
         for q in range(4):
             nc.gpsimd.dma_start(
-                out=planes[32 * q : 32 * q + 4, 6, :].bitcast(F32), in_=U_w_scales[20, 4 * q : 4 * q + 4, :].bitcast(F32)
+                out=late[32 * q : 32 * q + 4, 6 - HWT, :].bitcast(F32), in_=U_w_scales[20, 4 * q : 4 * q + 4, :].bitcast(F32)
             )
 
         a_codes = keep.tile([P, GROUPS * P], U32, align_bytes=64)
@@ -143,12 +145,14 @@ def tile_recurrentsig_w_kernel(
 
         def mx_pass(g, c, rhs):
             k = 4 * (g % 4)
+            t = g // 4
+            plane = planes[k:P, t, CH * c : CH * (c + 1)] if t < HWT else late[k:P, t - HWT, CH * c : CH * (c + 1)]
             nc.tensor.matmul_mx(
                 out=z[c][:],
                 lhsT=a_codes[:, P * g : P * (g + 1)].bitcast(FP8X4),
                 lhsT_scale=a_scales[:, P * g : P * (g + 1)],
                 rhs=rhs.bitcast(FP8X4),
-                rhs_scale=planes[k:P, g // 4, CH * c : CH * (c + 1)],
+                rhs_scale=plane,
                 start=(g == 0),
                 stop=(g == GROUPS - 1),
             )

@@ -21,10 +21,9 @@ GROUPS = KTOT // 512
 WG = IN // 512
 CH = 512
 NCH = UNITS // CH
-TAILG = 12
+TAILG = 18
 PERT = 3
 FULLG = GROUPS - TAILG
-HWT = 3
 LOOK = 8
 FLOPS = 2 * P * KTOT * UNITS
 
@@ -40,16 +39,14 @@ def tile_recurrentsig_w_kernel(
         tpool = ctx.enter_context(tc.psum_pool(name="tpool", bufs=5))
         zpool = ctx.enter_context(tc.psum_pool(name="zpool", bufs=1))
 
-        bias_rows = keep.tile([P, UNITS], BF16)
-        nc.vector.memset(bias_rows[:], 0.0)
-        planes = keep.tile([P, HWT, UNITS], U8, align_bytes=64)
+        planes = keep.tile([P, 7, UNITS], U8, align_bytes=64)
         nc.vector.memset(planes[:].rearrange("p t n -> p (t n)").bitcast(I32), 0)
-        late = keep.tile([P, 7 - HWT, UNITS], U8, align_bytes=64)
-        nc.vector.memset(late[:].rearrange("p t n -> p (t n)").bitcast(I32), 0)
-        ones = keep.tile([P, P], BF16)
-        nc.vector.memset(ones[:], 1.0)
         ident = keep.tile([P, P], F32)
         make_identity(nc, ident[:])
+        ones = keep.tile([P, P], BF16)
+        nc.gpsimd.memset(ones[:], 1.0)
+        bias_rows = keep.tile([P, UNITS], BF16)
+        nc.gpsimd.memset(bias_rows[:], 0.0)
         ltl = keep.tile([P, 1], BF16)
         nc.scalar.dma_start(out=ltl[:], in_=log_timelapse.partition_broadcast(P))
         nc.scalar.dma_start(out=bias_rows[0:1, :], in_=W_b.rearrange("(o n) -> o n", o=1))
@@ -65,23 +62,18 @@ def tile_recurrentsig_w_kernel(
         sigs = acts[:, IN : IN + UNITS * SIG].rearrange("p (n j) -> p n j", j=SIG)
         states = acts[:, IN + UNITS * SIG : KTOT]
 
-        for t in range(HWT):
+        for t in range(7):
             for q in range(4):
                 if t == 0:
                     src = W_w_scales[0:4, 4 * q : 4 * q + 4, :]
-                else:
+                    rows = 16
+                elif t < 6:
                     src = U_w_scales[4 * (t - 1) : 4 * t, 4 * q : 4 * q + 4, :]
-                nc.sync.dma_start(out=planes[32 * q : 32 * q + 16, t, :].bitcast(I32), in_=src.bitcast(I32))
-        by_row = U_w_scales[4 * (HWT - 1) : 20].rearrange("(t k) q n -> q k t n", k=4)
-        for q in range(4):
-            for r in range(4):
-                nc.gpsimd.dma_start(
-                    out=late[32 * q + r : 32 * q + 16 : 4, 0 : 6 - HWT, :].bitcast(F32), in_=by_row[4 * q + r].bitcast(F32)
-                )
-        for q in range(4):
-            nc.gpsimd.dma_start(
-                out=late[32 * q : 32 * q + 4, 6 - HWT, :].bitcast(F32), in_=U_w_scales[20, 4 * q : 4 * q + 4, :].bitcast(F32)
-            )
+                    rows = 16
+                else:
+                    src = U_w_scales[20, 4 * q : 4 * q + 4, :]
+                    rows = 4
+                nc.sync.dma_start(out=planes[32 * q : 32 * q + rows, t, :].bitcast(I32), in_=src.bitcast(I32))
 
         a_codes = keep.tile([P, GROUPS * P], U32, align_bytes=64)
         a_scales = keep.tile([P, GROUPS * P], U8, align_bytes=64)
@@ -145,14 +137,12 @@ def tile_recurrentsig_w_kernel(
 
         def mx_pass(g, c, rhs):
             k = 4 * (g % 4)
-            t = g // 4
-            plane = planes[k:P, t, CH * c : CH * (c + 1)] if t < HWT else late[k:P, t - HWT, CH * c : CH * (c + 1)]
             nc.tensor.matmul_mx(
                 out=z[c][:],
                 lhsT=a_codes[:, P * g : P * (g + 1)].bitcast(FP8X4),
                 lhsT_scale=a_scales[:, P * g : P * (g + 1)],
                 rhs=rhs.bitcast(FP8X4),
-                rhs_scale=plane,
+                rhs_scale=planes[k:P, g // 4, CH * c : CH * (c + 1)],
                 start=(g == 0),
                 stop=(g == GROUPS - 1),
             )

@@ -21,9 +21,10 @@ GROUPS = KTOT // 512
 WG = IN // 512
 CH = 512
 NCH = UNITS // CH
-TAILG = 18
+TAILG = 12
 PERT = 3
 FULLG = GROUPS - TAILG
+HWT = 3
 LOOK = 8
 FLOPS = 2 * P * KTOT * UNITS
 
@@ -39,14 +40,16 @@ def tile_recurrentsig_w_kernel(
         tpool = ctx.enter_context(tc.psum_pool(name="tpool", bufs=5))
         zpool = ctx.enter_context(tc.psum_pool(name="zpool", bufs=1))
 
-        planes = keep.tile([P, 7, UNITS], U8, align_bytes=64)
+        bias_rows = keep.tile([P, UNITS], BF16)
+        nc.vector.memset(bias_rows[:], 0.0)
+        planes = keep.tile([P, HWT, UNITS], U8, align_bytes=64)
         nc.vector.memset(planes[:].rearrange("p t n -> p (t n)").bitcast(I32), 0)
+        late = keep.tile([P, 7 - HWT, UNITS], U8, align_bytes=64)
+        nc.vector.memset(late[:].rearrange("p t n -> p (t n)").bitcast(I32), 0)
+        ones = keep.tile([P, P], BF16)
+        nc.vector.memset(ones[:], 1.0)
         ident = keep.tile([P, P], F32)
         make_identity(nc, ident[:])
-        ones = keep.tile([P, P], BF16)
-        nc.gpsimd.memset(ones[:], 1.0)
-        bias_rows = keep.tile([P, UNITS], BF16)
-        nc.gpsimd.memset(bias_rows[:], 0.0)
         ltl = keep.tile([P, 1], BF16)
         nc.scalar.dma_start(out=ltl[:], in_=log_timelapse.partition_broadcast(P))
         nc.scalar.dma_start(out=bias_rows[0:1, :], in_=W_b.rearrange("(o n) -> o n", o=1))
@@ -62,18 +65,23 @@ def tile_recurrentsig_w_kernel(
         sigs = acts[:, IN : IN + UNITS * SIG].rearrange("p (n j) -> p n j", j=SIG)
         states = acts[:, IN + UNITS * SIG : KTOT]
 
-        for t in range(7):
+        for t in range(HWT):
             for q in range(4):
                 if t == 0:
                     src = W_w_scales[0:4, 4 * q : 4 * q + 4, :]
-                    rows = 16
-                elif t < 6:
-                    src = U_w_scales[4 * (t - 1) : 4 * t, 4 * q : 4 * q + 4, :]
-                    rows = 16
                 else:
-                    src = U_w_scales[20, 4 * q : 4 * q + 4, :]
-                    rows = 4
-                nc.sync.dma_start(out=planes[32 * q : 32 * q + rows, t, :].bitcast(I32), in_=src.bitcast(I32))
+                    src = U_w_scales[4 * (t - 1) : 4 * t, 4 * q : 4 * q + 4, :]
+                nc.sync.dma_start(out=planes[32 * q : 32 * q + 16, t, :].bitcast(I32), in_=src.bitcast(I32))
+        by_row = U_w_scales[4 * (HWT - 1) : 20].rearrange("(t k) q n -> q k t n", k=4)
+        for q in range(4):
+            for r in range(4):
+                nc.gpsimd.dma_start(
+                    out=late[32 * q + r : 32 * q + 16 : 4, 0 : 6 - HWT, :].bitcast(F32), in_=by_row[4 * q + r].bitcast(F32)
+                )
+        for q in range(4):
+            nc.gpsimd.dma_start(
+                out=late[32 * q : 32 * q + 4, 6 - HWT, :].bitcast(F32), in_=U_w_scales[20, 4 * q : 4 * q + 4, :].bitcast(F32)
+            )
 
         a_codes = keep.tile([P, GROUPS * P], U32, align_bytes=64)
         a_scales = keep.tile([P, GROUPS * P], U8, align_bytes=64)
@@ -98,10 +106,7 @@ def tile_recurrentsig_w_kernel(
             grouped = stage.tile([P, 2, P, 4], BF16, align_bytes=64, tag="grouped")
             dst = grouped[:, 0:ng].bitcast(F32)
             src = tp[:, 0:ng].rearrange("p g u b -> p g b u")
-            if i % 2 == 0:
-                nc.vector.tensor_copy(out=dst, in_=src)
-            else:
-                nc.scalar.copy(out=dst, in_=src)
+            nc.vector.tensor_copy(out=dst, in_=src)
             regrouped.append((ng, grouped))
             if i > 0:
                 quantise(i - 1)
@@ -137,12 +142,14 @@ def tile_recurrentsig_w_kernel(
 
         def mx_pass(g, c, rhs):
             k = 4 * (g % 4)
+            t = g // 4
+            plane = planes[k:P, t, CH * c : CH * (c + 1)] if t < HWT else late[k:P, t - HWT, CH * c : CH * (c + 1)]
             nc.tensor.matmul_mx(
                 out=z[c][:],
                 lhsT=a_codes[:, P * g : P * (g + 1)].bitcast(FP8X4),
                 lhsT_scale=a_scales[:, P * g : P * (g + 1)],
                 rhs=rhs.bitcast(FP8X4),
-                rhs_scale=planes[k:P, g // 4, CH * c : CH * (c + 1)],
+                rhs_scale=plane,
                 start=(g == 0),
                 stop=(g == GROUPS - 1),
             )

@@ -42,10 +42,8 @@ def tile_recurrentsig_w_kernel(
 
         bias_rows = keep.tile([P, UNITS], BF16)
         nc.vector.memset(bias_rows[:], 0.0)
-        planes = keep.tile([P, HWT, UNITS], U8, align_bytes=64)
+        planes = keep.tile([P, 7, UNITS], U8, align_bytes=64)
         nc.vector.memset(planes[:].rearrange("p t n -> p (t n)").bitcast(I32), 0)
-        late = keep.tile([P, 7 - HWT, UNITS], U8, align_bytes=64)
-        nc.vector.memset(late[:].rearrange("p t n -> p (t n)").bitcast(I32), 0)
         ones = keep.tile([P, P], BF16)
         nc.vector.memset(ones[:], 1.0)
         ident = keep.tile([P, P], F32)
@@ -76,11 +74,11 @@ def tile_recurrentsig_w_kernel(
         for q in range(4):
             for r in range(4):
                 nc.gpsimd.dma_start(
-                    out=late[32 * q + r : 32 * q + 16 : 4, 0 : 6 - HWT, :].bitcast(F32), in_=by_row[4 * q + r].bitcast(F32)
+                    out=planes[32 * q + r : 32 * q + 16 : 4, HWT:6, :].bitcast(F32), in_=by_row[4 * q + r].bitcast(F32)
                 )
         for q in range(4):
             nc.gpsimd.dma_start(
-                out=late[32 * q : 32 * q + 4, 6 - HWT, :].bitcast(F32), in_=U_w_scales[20, 4 * q : 4 * q + 4, :].bitcast(F32)
+                out=planes[32 * q : 32 * q + 4, 6, :].bitcast(F32), in_=U_w_scales[20, 4 * q : 4 * q + 4, :].bitcast(F32)
             )
 
         a_codes = keep.tile([P, GROUPS * P], U32, align_bytes=64)
@@ -106,7 +104,10 @@ def tile_recurrentsig_w_kernel(
             grouped = stage.tile([P, 2, P, 4], BF16, align_bytes=64, tag="grouped")
             dst = grouped[:, 0:ng].bitcast(F32)
             src = tp[:, 0:ng].rearrange("p g u b -> p g b u")
-            nc.vector.tensor_copy(out=dst, in_=src)
+            if i % 2 == 0:
+                nc.vector.tensor_copy(out=dst, in_=src)
+            else:
+                nc.scalar.copy(out=dst, in_=src)
             regrouped.append((ng, grouped))
             if i > 0:
                 quantise(i - 1)
@@ -116,69 +117,69 @@ def tile_recurrentsig_w_kernel(
         nc.scalar.activation(out=tl[:], in_=ltl[:], func=ACT.Exp)
         tlh = keep.tile([P, 1], F32)
         nc.scalar.mul(out=tlh[:], in_=tl[:], mul=0.5)
-        bias_b = keep.tile([P, UNITS], F32)
-        for c in range(NCH):
-            bp = tpool.tile([P, CH], F32, tag="tp")
-            nc.tensor.matmul(out=bp[:], lhsT=ones[:], rhs=bias_rows[:, CH * c : CH * (c + 1)], start=True, stop=True)
-            nc.scalar.copy(out=bias_b[:, CH * c : CH * (c + 1)], in_=bp[:])
-        vps, wps, pps = [], [], []
+        base2 = keep.tile([P, 2, UNITS], F32)
         for c in range(NCH):
             cols = slice(CH * c, CH * (c + 1))
-            vp = keep.tile([P, 2, CH], F32, name="vp%d" % c)
-            wp = keep.tile([P, 2, CH], F32, name="wp%d" % c)
-            pp = keep.tile([P, 3, CH, 2], F32, name="pp%d" % c)
-            nc.scalar.activation(out=wp[:, 1, :], in_=sigs[:, cols, 1], func=ACT.Identity, bias=tlh[:, 0:1], scale=1.0)
-            nc.scalar.activation(out=vp[:, 1, :], in_=sigs[:, cols, 1], func=ACT.Identity, bias=tl[:, 0:1], scale=0.0)
-            nc.scalar.activation(
-                out=pp[:, 0, :, 1], in_=sigs[:, cols, 1], func=ACT.Identity, bias=tl[:, 0:1], scale=0.0
-            )
-            vps.append(vp)
-            wps.append(wp)
-            pps.append(pp)
+            bp = tpool.tile([P, CH], F32, tag="tp")
+            nc.tensor.matmul(out=bp[:], lhsT=ones[:], rhs=bias_rows[:, cols], start=True, stop=True)
+            nc.scalar.copy(out=base2[:, 0, cols], in_=bp[:])
+            nc.vector.tensor_tensor(out=base2[:, 1, cols], in0=bp[:], in1=states[:, cols], op=ALU.subtract)
+        twice0 = keep.tile([P, UNITS], F32)
+        nc.vector.scalar_tensor_tensor(
+            out=twice0[:], in0=sigs[:, :, 0], scalar=2.0, in1=base2[:, 1, :], op0=ALU.mult, op1=ALU.add
+        )
+        wqs = []
+        for c in range(NCH):
+            cols = slice(CH * c, CH * (c + 1))
+            wq = keep.tile([P, 3, CH], F32, name="wq%d" % c)
+            nc.gpsimd.memset(wq[:, 0, :], 2.0)
+            nc.scalar.activation(out=wq[:, 2, :], in_=sigs[:, cols, 1], func=ACT.Identity, bias=tl[:, 0:1], scale=2.0)
+            wqs.append(wq)
         sig4 = acts[:, IN : IN + UNITS * SIG].rearrange("p (n k e) -> p n k e", k=3, e=2)
 
         z = [zpool.tile([P, CH], F32, name="z%d" % c) for c in range(NCH)]
-        rout = keep.tile([P, UNITS], F32)
+        rd = keep.tile([P, 2, UNITS], F32)
 
         def mx_pass(g, c, rhs):
             k = 4 * (g % 4)
-            t = g // 4
-            plane = planes[k:P, t, CH * c : CH * (c + 1)] if t < HWT else late[k:P, t - HWT, CH * c : CH * (c + 1)]
             nc.tensor.matmul_mx(
                 out=z[c][:],
                 lhsT=a_codes[:, P * g : P * (g + 1)].bitcast(FP8X4),
                 lhsT_scale=a_scales[:, P * g : P * (g + 1)],
                 rhs=rhs.bitcast(FP8X4),
-                rhs_scale=plane,
+                rhs_scale=planes[k:P, g // 4, CH * c : CH * (c + 1)],
                 start=(g == 0),
                 stop=(g == GROUPS - 1),
             )
 
         def epilogue(c, parts):
-            vp, wp, pp = vps[c], wps[c], pps[c]
+            wq = wqs[c]
+            pp = stage.tile([P, 2, CH, 3], F32, tag="pp", bufs=2)
             osig = keep.tile([P, CH, 3, 2], F32, name="osig%d" % c)
             w = CH // parts
             whole = slice(CH * c, CH * (c + 1))
-            nc.vector.tensor_tensor(out=rout[:, whole], in0=z[c][:], in1=bias_b[:, whole], op=ALU.add)
-            nc.sync.dma_start(out=out[:, UNITS * SIG + CH * c : UNITS * SIG + CH * (c + 1)], in_=rout[:, whole])
+            nc.vector.tensor_tensor(out=wq[:, 1, :], in0=z[c][:], in1=twice0[:, whole], op=ALU.add)
+            nc.vector.tensor_tensor(
+                out=rd[:, :, whole], in0=z[c][:].unsqueeze(1).to_broadcast([P, 2, CH]), in1=base2[:, :, whole], op=ALU.add
+            )
+            if c == NCH - 1:
+                nc.sync.dma_start(out=out[:, UNITS * SIG : UNITS * (SIG + 1)], in_=rd[:, 0, :])
             for h in range(parts):
                 loc = slice(w * h, w * (h + 1))
                 cols = slice(CH * c + w * h, CH * c + w * (h + 1))
-                d = vp[:, 0, loc]
-                nc.vector.tensor_tensor(out=d, in0=rout[:, cols], in1=states[:, cols], op=ALU.subtract)
-                nc.scalar.copy(out=pp[:, 0, loc, 0], in_=d)
+                factors = wq[:, :, loc].rearrange("p i n -> p n i")
+                nc.scalar.activation(out=pp[:, 1, loc, :], in_=factors, func=ACT.Copy, scale=tlh[:, 0:1])
                 nc.vector.scalar_tensor_tensor(
-                    out=wp[:, 0, loc], in0=d, scalar=0.5, in1=sigs[:, cols, 0], op0=ALU.mult, op1=ALU.add
-                )
-                nc.vector.tensor_tensor(
-                    out=pp[:, 1:3, loc, :],
-                    in0=wp[:, :, loc].unsqueeze(3).to_broadcast([P, 2, w, 2]),
-                    in1=vp[:, :, loc].rearrange("p j n -> p n j").unsqueeze(1).to_broadcast([P, 2, w, 2]),
-                    op=ALU.mult,
+                    out=pp[:, 0, loc, :],
+                    in0=rd[:, 1, cols].unsqueeze(2).to_broadcast([P, w, 3]),
+                    scalar=0.5,
+                    in1=factors,
+                    op0=ALU.mult,
+                    op1=ALU.mult,
                 )
                 nc.vector.tensor_tensor(
                     out=osig[:, loc, :, :],
-                    in0=pp[:, :, loc, :].rearrange("p k n e -> p n k e"),
+                    in0=pp[:, :, loc, :].rearrange("p v n i -> p n i v"),
                     in1=sig4[:, cols, :, :],
                     op=ALU.add,
                 )

@@ -48,8 +48,9 @@ def tile_recurrentsig_w_kernel(
         nc.vector.memset(ones[:], 1.0)
         ident = keep.tile([P, P], F32)
         make_identity(nc, ident[:])
-        ltl = keep.tile([P, 1], BF16)
-        nc.scalar.dma_start(out=ltl[:], in_=log_timelapse.partition_broadcast(P))
+        lt_rows = keep.tile([P, 2], BF16)
+        nc.vector.memset(lt_rows[:], 0.0)
+        nc.scalar.dma_start(out=lt_rows[0:1, 0:1], in_=log_timelapse.rearrange("(o n) -> o n", o=1))
         nc.scalar.dma_start(out=bias_rows[0:1, :], in_=W_b.rearrange("(o n) -> o n", o=1))
         nc.scalar.dma_start(out=bias_rows[1:2, :], in_=U_b.rearrange("(o n) -> o n", o=1))
 
@@ -114,7 +115,9 @@ def tile_recurrentsig_w_kernel(
         quantise((GROUPS + 1) // 2 - 1)
 
         tl = keep.tile([P, 1], F32)
-        nc.scalar.activation(out=tl[:], in_=ltl[:], func=ACT.Exp)
+        lp = tpool.tile([P, CH], F32, tag="tp")
+        nc.tensor.matmul(out=lp[:, 0:2], lhsT=ones[:], rhs=lt_rows[:], start=True, stop=True)
+        nc.scalar.activation(out=tl[:], in_=lp[:, 0:1], func=ACT.Exp)
         tlh = keep.tile([P, 1], F32)
         nc.scalar.mul(out=tlh[:], in_=tl[:], mul=0.5)
         base2 = keep.tile([P, 2, UNITS], F32)

@@ -24,7 +24,6 @@ NCH = UNITS // CH
 TAILG = 12
 PERT = 3
 FULLG = GROUPS - TAILG
-HWT = 3
 LOOK = 8
 FLOPS = 2 * P * KTOT * UNITS
 
@@ -64,23 +63,14 @@ def tile_recurrentsig_w_kernel(
         sigs = acts[:, IN : IN + UNITS * SIG].rearrange("p (n j) -> p n j", j=SIG)
         states = acts[:, IN + UNITS * SIG : KTOT]
 
-        for t in range(HWT):
+        for t in range((GROUPS + 3) // 4):
+            ng = min(4, GROUPS - 4 * t)
             for q in range(4):
                 if t == 0:
                     src = W_w_scales[0:4, 4 * q : 4 * q + 4, :]
                 else:
-                    src = U_w_scales[4 * (t - 1) : 4 * t, 4 * q : 4 * q + 4, :]
-                nc.sync.dma_start(out=planes[32 * q : 32 * q + 16, t, :].bitcast(I32), in_=src.bitcast(I32))
-        by_row = U_w_scales[4 * (HWT - 1) : 20].rearrange("(t k) q n -> q k t n", k=4)
-        for q in range(4):
-            for r in range(4):
-                nc.gpsimd.dma_start(
-                    out=planes[32 * q + r : 32 * q + 16 : 4, HWT:6, :].bitcast(F32), in_=by_row[4 * q + r].bitcast(F32)
-                )
-        for q in range(4):
-            nc.gpsimd.dma_start(
-                out=planes[32 * q : 32 * q + 4, 6, :].bitcast(F32), in_=U_w_scales[20, 4 * q : 4 * q + 4, :].bitcast(F32)
-            )
+                    src = U_w_scales[4 * (t - 1) : 4 * (t - 1) + ng, 4 * q : 4 * q + 4, :]
+                nc.gpsimd.dma_start(out=planes[32 * q : 32 * q + 4 * ng, t, :].bitcast(F32), in_=src.bitcast(F32))
 
         a_codes = keep.tile([P, GROUPS * P], U32, align_bytes=64)
         a_scales = keep.tile([P, GROUPS * P], U8, align_bytes=64)

@@ -21,7 +21,7 @@ GROUPS = KTOT // 512
 WG = IN // 512
 CH = 512
 NCH = UNITS // CH
-TAILG = 12
+TAILG = 15
 PERT = 3
 FULLG = GROUPS - TAILG
 LOOK = 8
@@ -145,6 +145,16 @@ def tile_recurrentsig_w_kernel(
                 stop=(g == GROUPS - 1),
             )
 
+        pending = []
+
+        def store(dst, src):
+            pending.append((dst, src))
+
+        def flush():
+            for dst, src in pending:
+                nc.sync.dma_start(out=dst, in_=src)
+            pending.clear()
+
         def epilogue(c, parts):
             wq = wqs[c]
             pp = stage.tile([P, 2, CH, 3], F32, tag="pp", bufs=2)
@@ -156,7 +166,7 @@ def tile_recurrentsig_w_kernel(
                 out=rd[:, :, whole], in0=z[c][:].unsqueeze(1).to_broadcast([P, 2, CH]), in1=base2[:, :, whole], op=ALU.add
             )
             if c == NCH - 1:
-                nc.sync.dma_start(out=out[:, UNITS * SIG : UNITS * (SIG + 1)], in_=rd[:, 0, :])
+                store(out[:, UNITS * SIG : UNITS * (SIG + 1)], rd[:, 0, :])
             for h in range(parts):
                 loc = slice(w * h, w * (h + 1))
                 cols = slice(CH * c + w * h, CH * c + w * (h + 1))
@@ -176,9 +186,9 @@ def tile_recurrentsig_w_kernel(
                     in1=sig4[:, cols, :, :],
                     op=ALU.add,
                 )
-                nc.sync.dma_start(
-                    out=out[:, SIG * (CH * c + w * h) : SIG * (CH * c + w * (h + 1))],
-                    in_=osig[:, loc, :, :].rearrange("p n k e -> p (n k e)"),
+                store(
+                    out[:, SIG * (CH * c + w * h) : SIG * (CH * c + w * (h + 1))],
+                    osig[:, loc, :, :].rearrange("p n k e -> p (n k e)"),
                 )
 
         plan = [("full", g, 0) for g in range(FULLG)]
@@ -215,3 +225,5 @@ def tile_recurrentsig_w_kernel(
                     mx_pass(g + gi, c, tiles[i][:, gi, :])
                 if g + PERT == GROUPS:
                     epilogue(c, 2 if c == NCH - 1 else 1)
+            if i + LOOK >= len(plan) - 1:
+                flush()

@@ -41,7 +41,7 @@ def tile_recurrentsig_w_kernel(
 
         bias_rows = keep.tile([P, UNITS], BF16)
         nc.vector.memset(bias_rows[:], 0.0)
-        planes = keep.tile([P, 7, UNITS], U8, align_bytes=64)
+        planes = keep.tile([P, 7, UNITS], U8, align_bytes=256)
         nc.vector.memset(planes[:].rearrange("p t n -> p (t n)").bitcast(I32), 0)
         ones = keep.tile([P, P], BF16)
         nc.vector.memset(ones[:], 1.0)
@@ -53,7 +53,7 @@ def tile_recurrentsig_w_kernel(
         nc.scalar.dma_start(out=bias_rows[0:1, :], in_=W_b.rearrange("(o n) -> o n", o=1))
         nc.scalar.dma_start(out=bias_rows[1:2, :], in_=U_b.rearrange("(o n) -> o n", o=1))
 
-        acts = keep.tile([P, KTOT], BF16, align_bytes=64)
+        acts = keep.tile([P, KTOT], BF16, align_bytes=256)
         nc.sync.dma_start(out=acts[:, 0:IN], in_=x)
         for s in range(3):
             nc.sync.dma_start(
@@ -131,7 +131,7 @@ def tile_recurrentsig_w_kernel(
         sig4 = acts[:, IN : IN + UNITS * SIG].rearrange("p (n k e) -> p n k e", k=3, e=2)
 
         z = [zpool.tile([P, CH], F32, name="z%d" % c) for c in range(NCH)]
-        rd = keep.tile([P, 2, UNITS], F32)
+        rd = keep.tile([P, 2, UNITS], F32, align_bytes=256)
 
         def mx_pass(g, c, rhs):
             k = 4 * (g % 4)
@@ -158,7 +158,7 @@ def tile_recurrentsig_w_kernel(
         def epilogue(c, parts):
             wq = wqs[c]
             pp = stage.tile([P, 2, CH, 3], F32, tag="pp", bufs=2)
-            osig = keep.tile([P, CH, 3, 2], F32, name="osig%d" % c)
+            osig = keep.tile([P, CH, 3, 2], F32, name="osig%d" % c, align_bytes=256)
             w = CH // parts
             whole = slice(CH * c, CH * (c + 1))
             nc.vector.tensor_tensor(out=wq[:, 1, :], in0=z[c][:], in1=twice0[:, whole], op=ALU.add)
@@ -198,11 +198,11 @@ def tile_recurrentsig_w_kernel(
         def load(i):
             kind, g, c = plan[i]
             if kind == "full":
-                wt = wpool.tile([P, UNITS], U32, align_bytes=64, tag="wt")
+                wt = wpool.tile([P, UNITS], U32, align_bytes=256, tag="wt")
                 words = W_w_words[g] if g < WG else U_w_words[g - WG]
                 nc.sync.dma_start(out=wt[:].bitcast(I32), in_=words.rearrange("p n t -> p (n t)").bitcast(I32))
             else:
-                wt = wpool.tile([P, PERT, CH], U32, align_bytes=64, tag="wt")
+                wt = wpool.tile([P, PERT, CH], U32, align_bytes=256, tag="wt")
                 nc.sync.dma_start(
                     out=wt[:].bitcast(I32),
                     in_=U_w_words[g - WG : g - WG + PERT, :, CH * c : CH * (c + 1), :]

@@ -155,11 +155,10 @@ def tile_recurrentsig_w_kernel(
                 nc.sync.dma_start(out=dst, in_=src)
             pending.clear()
 
-        def epilogue(c, parts):
+        def epilogue(c, widths):
             wq = wqs[c]
             pp = stage.tile([P, 2, CH, 3], F32, tag="pp", bufs=2)
             osig = keep.tile([P, CH, 3, 2], F32, name="osig%d" % c, align_bytes=256)
-            w = CH // parts
             whole = slice(CH * c, CH * (c + 1))
             nc.vector.tensor_tensor(out=wq[:, 1, :], in0=z[c][:], in1=twice0[:, whole], op=ALU.add)
             nc.vector.tensor_tensor(
@@ -167,9 +166,12 @@ def tile_recurrentsig_w_kernel(
             )
             if c == NCH - 1:
                 store(out[:, UNITS * SIG : UNITS * (SIG + 1)], rd[:, 0, :])
-            for h in range(parts):
-                loc = slice(w * h, w * (h + 1))
-                cols = slice(CH * c + w * h, CH * c + w * (h + 1))
+            starts = [sum(widths[0:h]) for h in range(len(widths))]
+
+            def products(h):
+                w = widths[h]
+                loc = slice(starts[h], starts[h] + w)
+                cols = slice(CH * c + starts[h], CH * c + starts[h] + w)
                 factors = wq[:, :, loc].rearrange("p i n -> p n i")
                 nc.scalar.activation(out=pp[:, 1, loc, :], in_=factors, func=ACT.Copy, scale=tlh[:, 0:1])
                 nc.vector.scalar_tensor_tensor(
@@ -180,6 +182,11 @@ def tile_recurrentsig_w_kernel(
                     op0=ALU.mult,
                     op1=ALU.mult,
                 )
+
+            def finish(h):
+                w = widths[h]
+                loc = slice(starts[h], starts[h] + w)
+                cols = slice(CH * c + starts[h], CH * c + starts[h] + w)
                 nc.vector.tensor_tensor(
                     out=osig[:, loc, :, :],
                     in0=pp[:, :, loc, :].rearrange("p v n i -> p n i v"),
@@ -187,16 +194,26 @@ def tile_recurrentsig_w_kernel(
                     op=ALU.add,
                 )
                 store(
-                    out[:, SIG * (CH * c + w * h) : SIG * (CH * c + w * (h + 1))],
+                    out[:, SIG * (CH * c + starts[h]) : SIG * (CH * c + starts[h] + w)],
                     osig[:, loc, :, :].rearrange("p n k e -> p (n k e)"),
                 )
 
-        plan = [("full", g, 0) for g in range(FULLG)]
-        plan += [("tail", FULLG + PERT * j, c) for c in range(NCH) for j in range(TAILG // PERT)]
+            products(0)
+            for h in range(len(widths)):
+                if h + 1 < len(widths):
+                    products(h + 1)
+                finish(h)
+
+        plan = [("full", g, 1, 0) for g in range(FULLG)]
+        for c in range(NCH):
+            g = FULLG
+            for ng in (3, 3, 3, 3, 2, 1):
+                plan.append(("tail", g, ng, c))
+                g += ng
         tiles = []
 
         def load(i):
-            kind, g, c = plan[i]
+            kind, g, ng, c = plan[i]
             if kind == "full":
                 wt = wpool.tile([P, UNITS], U32, align_bytes=256, tag="wt")
                 words = W_w_words[g] if g < WG else U_w_words[g - WG]
@@ -204,8 +221,8 @@ def tile_recurrentsig_w_kernel(
             else:
                 wt = wpool.tile([P, PERT, CH], U32, align_bytes=256, tag="wt")
                 nc.sync.dma_start(
-                    out=wt[:].bitcast(I32),
-                    in_=U_w_words[g - WG : g - WG + PERT, :, CH * c : CH * (c + 1), :]
+                    out=wt[:, 0:ng, :].bitcast(I32),
+                    in_=U_w_words[g - WG : g - WG + ng, :, CH * c : CH * (c + 1), :]
                     .rearrange("g p n t -> p g (n t)")
                     .bitcast(I32),
                 )
@@ -216,14 +233,14 @@ def tile_recurrentsig_w_kernel(
         for i in range(len(plan)):
             if i + LOOK < len(plan):
                 load(i + LOOK)
-            kind, g, c = plan[i]
+            kind, g, ng, c = plan[i]
             if kind == "full":
                 for cc in range(NCH):
                     mx_pass(g, cc, tiles[i][:, CH * cc : CH * (cc + 1)])
             else:
-                for gi in range(PERT):
+                for gi in range(ng):
                     mx_pass(g + gi, c, tiles[i][:, gi, :])
-                if g + PERT == GROUPS:
-                    epilogue(c, 2 if c == NCH - 1 else 1)
+                if g + ng == GROUPS:
+                    epilogue(c, [256, 128, 128] if c == NCH - 1 else [CH])
             if i + LOOK >= len(plan) - 1:
                 flush()

@@ -21,7 +21,7 @@ GROUPS = KTOT // 512
 WG = IN // 512
 CH = 512
 NCH = UNITS // CH
-TAILG = 15
+TAILG = 21
 PERT = 3
 FULLG = GROUPS - TAILG
 LOOK = 8
@@ -207,7 +207,7 @@ def tile_recurrentsig_w_kernel(
         plan = [("full", g, 1, 0) for g in range(FULLG)]
         for c in range(NCH):
             g = FULLG
-            for ng in (3, 3, 3, 3, 2, 1):
+            for ng in (3, 3, 3, 3, 3, 3, 2, 1):
                 plan.append(("tail", g, ng, c))
                 g += ng
         tiles = []

@@ -65,12 +65,15 @@ def tile_recurrentsig_w_kernel(
 
         for t in range((GROUPS + 3) // 4):
             ng = min(4, GROUPS - 4 * t)
-            for q in range(4):
+            wide = 1 <= t and 4 * t + 8 <= GROUPS
+            for q in (0, 2, 1, 3) if wide else range(4):
                 if t == 0:
                     src = W_w_scales[0:4, 4 * q : 4 * q + 4, :]
                 else:
-                    src = U_w_scales[4 * (t - 1) : 4 * (t - 1) + ng, 4 * q : 4 * q + 4, :]
-                nc.gpsimd.dma_start(out=planes[32 * q : 32 * q + 4 * ng, t, :].bitcast(F32), in_=src.bitcast(F32))
+                    n = 8 if wide else ng
+                    src = U_w_scales[4 * (t - 1) : 4 * (t - 1) + n, 4 * q : 4 * q + 4, :]
+                rows = 32 if wide else 4 * ng
+                nc.gpsimd.dma_start(out=planes[32 * q : 32 * q + rows, t, :].bitcast(F32), in_=src.bitcast(F32))
 
         a_codes = keep.tile([P, GROUPS * P], U32, align_bytes=64)
         a_scales = keep.tile([P, GROUPS * P], U8, align_bytes=64)

@@ -21,10 +21,8 @@ GROUPS = KTOT // 512
 WG = IN // 512
 CH = 512
 NCH = UNITS // CH
-TAILG = 21
-PERT = 3
-FULLG = GROUPS - TAILG
-LOOK = 8
+WBUF = 2048
+LOOK = 7
 FLOPS = 2 * P * KTOT * UNITS
 
 
@@ -35,7 +33,7 @@ def tile_recurrentsig_w_kernel(
     with ExitStack() as ctx:
         keep = ctx.enter_context(tc.tile_pool(name="keep", bufs=1))
         stage = ctx.enter_context(tc.tile_pool(name="stage", bufs=4))
-        wpool = ctx.enter_context(tc.tile_pool(name="wpool", bufs=9))
+        wpool = ctx.enter_context(tc.tile_pool(name="wpool", bufs=LOOK + 1))
         tpool = ctx.enter_context(tc.psum_pool(name="tpool", bufs=5))
         zpool = ctx.enter_context(tc.psum_pool(name="zpool", bufs=1))
 
@@ -207,43 +205,37 @@ def tile_recurrentsig_w_kernel(
                     products(h + 1)
                 finish(h)
 
-        plan = [("full", g, 1, 0) for g in range(FULLG)]
-        for c in range(NCH):
-            g = FULLG
-            for ng in (3, 3, 3, 3, 3, 3, 2, 1):
-                plan.append(("tail", g, ng, c))
-                g += ng
+        plan = [(g, 2, 0, 2) for g in range(0, WG, 2)]
+        plan += [(g, 2, 0, 2) for g in range(WG, GROUPS - 3, 2)]
+        plan += [(GROUPS - 3, 3, c, 1) for c in range(2)]
+        g = 0
+        for ng in (4, 4, 4, 4, 4, 2, 2, 1):
+            plan.append((g, ng, 2, 1))
+            g += ng
         tiles = []
 
         def load(i):
-            kind, g, ng, c = plan[i]
-            if kind == "full":
-                wt = wpool.tile([P, UNITS], U32, align_bytes=256, tag="wt")
-                words = W_w_words[g] if g < WG else U_w_words[g - WG]
-                nc.sync.dma_start(out=wt[:].bitcast(I32), in_=words.rearrange("p n t -> p (n t)").bitcast(I32))
-            else:
-                wt = wpool.tile([P, PERT, CH], U32, align_bytes=256, tag="wt")
-                nc.sync.dma_start(
-                    out=wt[:, 0:ng, :].bitcast(I32),
-                    in_=U_w_words[g - WG : g - WG + ng, :, CH * c : CH * (c + 1), :]
-                    .rearrange("g p n t -> p g (n t)")
-                    .bitcast(I32),
-                )
-            tiles.append(wt)
+            g, ng, c, chunks = plan[i]
+            w = CH * chunks
+            wt = wpool.tile([P, WBUF], U32, align_bytes=256, tag="wt")
+            view = wt[:, 0 : ng * w].rearrange("p (g n) -> p g n", g=ng)
+            words = W_w_words[g : g + ng] if g < WG else U_w_words[g - WG : g - WG + ng]
+            nc.sync.dma_start(
+                out=view.bitcast(I32),
+                in_=words[:, :, CH * c : CH * c + w, :].rearrange("g p n t -> p g (n t)").bitcast(I32),
+            )
+            tiles.append(view)
 
         for i in range(LOOK):
             load(i)
         for i in range(len(plan)):
             if i + LOOK < len(plan):
                 load(i + LOOK)
-            kind, g, ng, c = plan[i]
-            if kind == "full":
-                for cc in range(NCH):
-                    mx_pass(g, cc, tiles[i][:, CH * cc : CH * (cc + 1)])
-            else:
-                for gi in range(ng):
-                    mx_pass(g + gi, c, tiles[i][:, gi, :])
-                if g + ng == GROUPS:
-                    epilogue(c, [256, 128, 128] if c == NCH - 1 else [CH])
+            g, ng, c, chunks = plan[i]
+            for gi in range(ng):
+                for cc in range(chunks):
+                    mx_pass(g + gi, c + cc, tiles[i][:, gi, CH * cc : CH * (cc + 1)])
+            if g + ng == GROUPS:
+                epilogue(c, [256, 128, 128] if c == NCH - 1 else [CH])
             if i + LOOK >= len(plan) - 1:
                 flush()

@@ -205,9 +205,9 @@ def tile_recurrentsig_w_kernel(
                     products(h + 1)
                 finish(h)
 
-        plan = [(g, 2, 0, 2) for g in range(0, WG, 2)]
-        plan += [(g, 2, 0, 2) for g in range(WG, GROUPS - 3, 2)]
-        plan += [(GROUPS - 3, 3, c, 1) for c in range(2)]
+        plan = [(g, 2, 0, 2) for g in range(0, GROUPS - 7, 2)]
+        for c in range(2):
+            plan += [(GROUPS - 7, 4, c, 1), (GROUPS - 3, 3, c, 1)]
         g = 0
         for ng in (4, 4, 4, 4, 4, 2, 2, 1):
             plan.append((g, ng, 2, 1))

from contextlib import ExitStack

import concourse.mybir as mybir
from concourse.masks import make_identity

F32 = mybir.dt.float32
BF16 = mybir.dt.bfloat16
I32 = mybir.dt.int32
U32 = mybir.dt.uint32
U8 = mybir.dt.uint8
FP8X4 = mybir.dt.float8_e4m3fn_x4
ALU = mybir.AluOpType
ACT = mybir.ActivationFunctionType

P = 128
IN = 2048
UNITS = 1536
SIG = 6
KTOT = IN + UNITS * (SIG + 1)
GROUPS = KTOT // 512
WG = IN // 512
CH = 512
NCH = UNITS // CH
WBUF = 2048
LOOK = 7
FLOPS = 2 * P * KTOT * UNITS


def tile_recurrentsig_w_kernel(
    tc, x, prev_sigs, prev_states, W_w_words, W_w_scales, W_b, U_w_words, U_w_scales, U_b, log_timelapse, out
):
    nc = tc.nc
    with ExitStack() as ctx:
        keep = ctx.enter_context(tc.tile_pool(name="keep", bufs=1))
        stage = ctx.enter_context(tc.tile_pool(name="stage", bufs=4))
        wpool = ctx.enter_context(tc.tile_pool(name="wpool", bufs=LOOK + 1))
        tpool = ctx.enter_context(tc.psum_pool(name="tpool", bufs=5))
        zpool = ctx.enter_context(tc.psum_pool(name="zpool", bufs=1))

        bias_rows = keep.tile([P, UNITS], BF16)
        nc.vector.memset(bias_rows[:], 0.0)
        planes = keep.tile([P, 7, UNITS], U8, align_bytes=256)
        nc.vector.memset(planes[:].rearrange("p t n -> p (t n)").bitcast(I32), 0)
        ones = keep.tile([P, P], BF16)
        nc.vector.memset(ones[:], 1.0)
        ident = keep.tile([P, P], F32)
        make_identity(nc, ident[:])
        lt_rows = keep.tile([P, 2], BF16)
        nc.vector.memset(lt_rows[:], 0.0)
        nc.scalar.dma_start(out=lt_rows[0:1, 0:1], in_=log_timelapse.rearrange("(o n) -> o n", o=1))
        nc.scalar.dma_start(out=bias_rows[0:1, :], in_=W_b.rearrange("(o n) -> o n", o=1))
        nc.scalar.dma_start(out=bias_rows[1:2, :], in_=U_b.rearrange("(o n) -> o n", o=1))

        acts = keep.tile([P, KTOT], BF16, align_bytes=256)
        nc.sync.dma_start(out=acts[:, 0:IN], in_=x)
        for s in range(3):
            nc.sync.dma_start(
                out=acts[:, IN + 3072 * s : IN + 3072 * (s + 1)], in_=prev_sigs[:, 3072 * s : 3072 * (s + 1)]
            )
        nc.sync.dma_start(out=acts[:, IN + UNITS * SIG : KTOT], in_=prev_states)
        sigs = acts[:, IN : IN + UNITS * SIG].rearrange("p (n j) -> p n j", j=SIG)
        states = acts[:, IN + UNITS * SIG : KTOT]

        for t in range((GROUPS + 3) // 4):
            ng = min(4, GROUPS - 4 * t)
            wide = 1 <= t and 4 * t + 8 <= GROUPS
            for q in (0, 2, 1, 3) if wide else range(4):
                if t == 0:
                    src = W_w_scales[0:4, 4 * q : 4 * q + 4, :]
                else:
                    n = 8 if wide else ng
                    src = U_w_scales[4 * (t - 1) : 4 * (t - 1) + n, 4 * q : 4 * q + 4, :]
                rows = 32 if wide else 4 * ng
                nc.gpsimd.dma_start(out=planes[32 * q : 32 * q + rows, t, :].bitcast(F32), in_=src.bitcast(F32))

        a_codes = keep.tile([P, GROUPS * P], U32, align_bytes=64)
        a_scales = keep.tile([P, GROUPS * P], U8, align_bytes=64)
        acts_w = acts[:].bitcast(F32)
        regrouped = []

        def quantise(i):
            ng, grouped = regrouped[i]
            nc.vector.quantize_mx(
                out=a_codes[:, 256 * i : 256 * i + P * ng].bitcast(FP8X4),
                scales=a_scales[:, 256 * i : 256 * i + P * ng],
                in_=grouped[:, 0:ng].rearrange("p g b t -> p (g b t)"),
            )

        for i in range((GROUPS + 1) // 2):
            ng = min(2, GROUPS - 2 * i)
            tp = tpool.tile([P, 2, 2, P], F32, tag="tp")
            for gi in range(ng):
                g = 2 * i + gi
                for u in range(2):
                    nc.tensor.transpose(tp[:, gi, u, :], acts_w[:, 256 * g + u : 256 * (g + 1) : 2], ident[:])
            grouped = stage.tile([P, 2, P, 4], BF16, align_bytes=64, tag="grouped")
            dst = grouped[:, 0:ng].bitcast(F32)
            src = tp[:, 0:ng].rearrange("p g u b -> p g b u")
            if i % 2 == 0:
                nc.vector.tensor_copy(out=dst, in_=src)
            else:
                nc.scalar.copy(out=dst, in_=src)
            regrouped.append((ng, grouped))
            if i > 0:
                quantise(i - 1)
        quantise((GROUPS + 1) // 2 - 1)

        tl = keep.tile([P, 1], F32)
        lp = tpool.tile([P, CH], F32, tag="tp")
        nc.tensor.matmul(out=lp[:, 0:2], lhsT=ones[:], rhs=lt_rows[:], start=True, stop=True)
        nc.scalar.activation(out=tl[:], in_=lp[:, 0:1], func=ACT.Exp)
        tlh = keep.tile([P, 1], F32)
        nc.scalar.mul(out=tlh[:], in_=tl[:], mul=0.5)
        base2 = keep.tile([P, 2, UNITS], F32)
        for c in range(NCH):
            cols = slice(CH * c, CH * (c + 1))
            bp = tpool.tile([P, CH], F32, tag="tp")
            nc.tensor.matmul(out=bp[:], lhsT=ones[:], rhs=bias_rows[:, cols], start=True, stop=True)
            nc.scalar.copy(out=base2[:, 0, cols], in_=bp[:])
            nc.vector.tensor_tensor(out=base2[:, 1, cols], in0=bp[:], in1=states[:, cols], op=ALU.subtract)
        twice0 = keep.tile([P, UNITS], F32)
        nc.vector.scalar_tensor_tensor(
            out=twice0[:], in0=sigs[:, :, 0], scalar=2.0, in1=base2[:, 1, :], op0=ALU.mult, op1=ALU.add
        )
        wqs = []
        for c in range(NCH):
            cols = slice(CH * c, CH * (c + 1))
            wq = keep.tile([P, 3, CH], F32, name="wq%d" % c)
            nc.gpsimd.memset(wq[:, 0, :], 2.0)
            nc.scalar.activation(out=wq[:, 2, :], in_=sigs[:, cols, 1], func=ACT.Identity, bias=tl[:, 0:1], scale=2.0)
            wqs.append(wq)
        sig4 = acts[:, IN : IN + UNITS * SIG].rearrange("p (n k e) -> p n k e", k=3, e=2)

        z = [zpool.tile([P, CH], F32, name="z%d" % c) for c in range(NCH)]
        rd = keep.tile([P, 2, UNITS], F32, align_bytes=256)

        def mx_pass(g, c, rhs):
            k = 4 * (g % 4)
            nc.tensor.matmul_mx(
                out=z[c][:],
                lhsT=a_codes[:, P * g : P * (g + 1)].bitcast(FP8X4),
                lhsT_scale=a_scales[:, P * g : P * (g + 1)],
                rhs=rhs.bitcast(FP8X4),
                rhs_scale=planes[k:P, g // 4, CH * c : CH * (c + 1)],
                start=(g == 0),
                stop=(g == GROUPS - 1),
            )

        pending = []

        def store(dst, src):
            pending.append((dst, src))

        def flush():
            for dst, src in pending:
                nc.sync.dma_start(out=dst, in_=src)
            pending.clear()

        def epilogue(c, widths):
            wq = wqs[c]
            pp = stage.tile([P, 2, CH, 3], F32, tag="pp", bufs=2)
            osig = keep.tile([P, CH, 3, 2], F32, name="osig%d" % c, align_bytes=256)
            whole = slice(CH * c, CH * (c + 1))
            nc.vector.tensor_tensor(out=wq[:, 1, :], in0=z[c][:], in1=twice0[:, whole], op=ALU.add)
            nc.vector.tensor_tensor(
                out=rd[:, :, whole], in0=z[c][:].unsqueeze(1).to_broadcast([P, 2, CH]), in1=base2[:, :, whole], op=ALU.add
            )
            if c == NCH - 1:
                store(out[:, UNITS * SIG : UNITS * (SIG + 1)], rd[:, 0, :])
            starts = [sum(widths[0:h]) for h in range(len(widths))]

            def products(h):
                w = widths[h]
                loc = slice(starts[h], starts[h] + w)
                cols = slice(CH * c + starts[h], CH * c + starts[h] + w)
                factors = wq[:, :, loc].rearrange("p i n -> p n i")
                nc.scalar.activation(out=pp[:, 1, loc, :], in_=factors, func=ACT.Copy, scale=tlh[:, 0:1])
                nc.vector.scalar_tensor_tensor(
                    out=pp[:, 0, loc, :],
                    in0=rd[:, 1, cols].unsqueeze(2).to_broadcast([P, w, 3]),
                    scalar=0.5,
                    in1=factors,
                    op0=ALU.mult,
                    op1=ALU.mult,
                )

            def finish(h):
                w = widths[h]
                loc = slice(starts[h], starts[h] + w)
                cols = slice(CH * c + starts[h], CH * c + starts[h] + w)
                nc.vector.tensor_tensor(
                    out=osig[:, loc, :, :],
                    in0=pp[:, :, loc, :].rearrange("p v n i -> p n i v"),
                    in1=sig4[:, cols, :, :],
                    op=ALU.add,
                )
                store(
                    out[:, SIG * (CH * c + starts[h]) : SIG * (CH * c + starts[h] + w)],
                    osig[:, loc, :, :].rearrange("p n k e -> p (n k e)"),
                )

            products(0)
            for h in range(len(widths)):
                if h + 1 < len(widths):
                    products(h + 1)
                finish(h)

        plan = [(g, 2, 0, 2) for g in range(0, GROUPS - 7, 2)]
        for c in range(2):
            plan += [(GROUPS - 7, 4, c, 1), (GROUPS - 3, 3, c, 1)]
        g = 0
        for ng in (4, 4, 4, 4, 4, 2, 2, 1):
            plan.append((g, ng, 2, 1))
            g += ng
        tiles = []

        def load(i):
            g, ng, c, chunks = plan[i]
            w = CH * chunks
            wt = wpool.tile([P, WBUF], U32, align_bytes=256, tag="wt")
            view = wt[:, 0 : ng * w].rearrange("p (g n) -> p g n", g=ng)
            words = W_w_words[g : g + ng] if g < WG else U_w_words[g - WG : g - WG + ng]
            nc.sync.dma_start(
                out=view.bitcast(I32),
                in_=words[:, :, CH * c : CH * c + w, :].rearrange("g p n t -> p g (n t)").bitcast(I32),
            )
            tiles.append(view)

        for i in range(LOOK):
            load(i)
        for i in range(len(plan)):
            if i + LOOK < len(plan):
                load(i + LOOK)
            g, ng, c, chunks = plan[i]
            for gi in range(ng):
                for cc in range(chunks):
                    mx_pass(g + gi, c + cc, tiles[i][:, gi, CH * cc : CH * (cc + 1)])
            if g + ng == GROUPS:
                epilogue(c, [256, 128, 128] if c == NCH - 1 else [CH])
            if i + LOOK >= len(plan) - 1:
                flush()
